import numpy as np
import ml_dtypes


def mxq(x, axis, fmt="e4m3"):
    dtype, down = {"e4m3": (ml_dtypes.float8_e4m3fn, 7), "e5m2": (ml_dtypes.float8_e5m2, 14)}[fmt]
    v = np.moveaxis(np.asarray(x, np.float32).astype(ml_dtypes.bfloat16).astype(np.float64), axis, -1)
    blocks = v.reshape(v.shape[:-1] + (-1, 32))
    amax = np.abs(blocks).max(-1, keepdims=True)
    byte = np.maximum(np.where(amax > 0, np.frexp(amax)[1] - 1 + 127, 0) - down, 1)
    scale = np.exp2(byte - 127.0)
    codes = (blocks / scale).astype(np.float32).astype(dtype).astype(np.float64)
    return np.moveaxis((codes * scale).reshape(v.shape), -1, axis)


WIDE = False


def mx_kscale(k):
    if not WIDE:
        return np.ones(k)
    levels = np.array([10, -10, 5, -5, 0])
    a = np.random.permutation(np.resize(levels, k // 512 * 4)).reshape(k // 512, 4)
    idx = np.arange(k)
    return np.exp2(a[idx // 512, idx % 128 // 32])


BF16 = ml_dtypes.bfloat16


def bf(x):
    return np.asarray(x, np.float32).astype(BF16)


def f64(x):
    return np.asarray(x).astype(np.float64)


B, S, DM, H, DH, QB = 1, 1024, 1024, 8, 256, 512
DI = H * DH
EPS_GN = 1e-5


def setup_inputs():
    s = mx_kscale(DI)
    h = np.random.standard_normal((B, S, H, DH)) * 0.15 + np.random.standard_normal((B, 1, H, 1)) * 0.15
    return {"h_attn": bf(h.reshape(B, S, DI)),
            "gn_w": bf((1.0 + 0.1 * np.random.standard_normal(DI)) * s),
            "gn_b": bf(0.1 * np.random.standard_normal(DI) * s),
            "W_out": bf(np.random.standard_normal((DM, DI)) / np.sqrt(DI) / s[None, :]),
            "x": bf(np.random.standard_normal((B, S, DM))),
            "skip_scale": bf(0.7 + 0.1 * np.random.standard_normal(1))}


def reference(h_attn, gn_w, gn_b, W_out, x, skip_scale):
    hg = f64(h_attn).reshape(B, S, H, DH)
    mu = hg.mean(axis=(1, 3), keepdims=True)
    var = hg.var(axis=(1, 3), keepdims=True)
    hg = (hg - mu) / np.sqrt(var + EPS_GN)
    h = hg.reshape(B, S, DI) * f64(gn_w) + f64(gn_b)
    return (mxq(h, 2, "e4m3") @ mxq(f64(W_out), 1, "e4m3").T) + f64(skip_scale) * f64(x)

@@ -1,0 +1,269 @@
+from contextlib import ExitStack
+
+import concourse.mybir as mybir
+from concourse.masks import make_identity
+
+F32 = mybir.dt.float32
+BF16 = mybir.dt.bfloat16
+U32 = mybir.dt.uint32
+U8 = mybir.dt.uint8
+FP8X4 = mybir.dt.float8_e4m3fn_x4
+ALU = mybir.AluOpType
+ACT = mybir.ActivationFunctionType
+
+P = 128
+PACK = 4
+K_PASS = P * PACK
+S = 1024
+DI = 2048
+DM = 1024
+GROUP = 256
+EPS_GN = 1e-5
+PASSES = DI // K_PASS
+GROUPS_PER_PASS = K_PASS // GROUP
+ROW_TILES = S // P
+W_TILES = DM // P
+N_TILE = 512
+N_HALVES = DM // N_TILE
+PSUM_BANKS = 8
+OPEN_TILES = PSUM_BANKS - 1
+
+FLOPS = 2 * S * DM * DI
+
+
+def tile_mlstmblock_pb_kernel(tc, h_attn, gn_w, gn_b, W_out, x, skip_scale, out):
+    nc = tc.nc
+    h_rows = h_attn.flatten_outer_dims().rearrange("(p j) c -> p j c", j=ROW_TILES)
+    x_rows = x.flatten_outer_dims().rearrange("(p j) m -> p j m", j=ROW_TILES)
+    out_rows = out.flatten_outer_dims().rearrange("(p j) m -> p j m", j=ROW_TILES)
+    w_rows = W_out.rearrange("(t p) c -> p t c", p=P)
+
+    with ExitStack() as ctx:
+        ctx.enter_context(tc.manual_schedule())
+        keep = ctx.enter_context(tc.tile_pool(name="keep", bufs=1))
+        small = ctx.enter_context(tc.tile_pool(name="small", bufs=2))
+        stage = ctx.enter_context(tc.tile_pool(name="stage", bufs=2))
+        results = ctx.enter_context(tc.tile_pool(name="results", bufs=4))
+        stats_bank = ctx.enter_context(tc.psum_pool(name="stats_bank", bufs=1))
+        psum = ctx.enter_context(tc.psum_pool(name="psum", bufs=PSUM_BANKS - 1))
+
+        params = keep.tile([P, 2 * P], BF16)
+        nc.vector.memset(params[:], 0.0)
+        nc.sync.dma_start(out=params[0:8, :], in_=gn_w.rearrange("(b c) -> b c", c=GROUP))
+        nc.sync.dma_start(out=params[8:16, :], in_=gn_b.rearrange("(b c) -> b c", c=GROUP))
+        skip_bf = keep.tile([P, 1], BF16)
+        nc.sync.dma_start(out=skip_bf[:], in_=skip_scale.partition_broadcast(P))
+        h_raw = [keep.tile([P, ROW_TILES, K_PASS], BF16, name="h_raw%d" % g) for g in range(PASSES)]
+        w_raw = [keep.tile([P, W_TILES, K_PASS], BF16, name="w_raw%d" % g) for g in range(PASSES)]
+        for g in range(PASSES):
+            nc.sync.dma_start(out=h_raw[g][:], in_=h_rows[:, :, g * K_PASS : (g + 1) * K_PASS])
+        for g in range(PASSES):
+            nc.sync.dma_start(out=w_raw[g][:], in_=w_rows[:, :, g * K_PASS : (g + 1) * K_PASS])
+        x_sb = keep.tile([P, ROW_TILES, DM], BF16)
+        nc.sync.dma_start(out=x_sb[:], in_=x_rows)
+
+        ident_f32 = keep.tile([P, P], F32)
+        make_identity(nc, ident_f32[:])
+        ident_bf = keep.tile([P, P], BF16)
+        make_identity(nc, ident_bf[:])
+        ones_bf = keep.tile([P, 2], BF16)
+        nc.vector.memset(ones_bf[:], 1.0)
+        minus_mean_of = keep.tile([P, P], F32)
+        nc.vector.memset(minus_mean_of[:], -1.0 / (S * GROUP))
+        mean_of = keep.tile([P, P], F32)
+        nc.vector.memset(mean_of[:], 1.0 / (S * GROUP))
+        minus_half = keep.tile([P, GROUPS_PER_PASS], F32)
+        nc.vector.memset(minus_half[:], -0.5)
+        skip = keep.tile([P, 1], F32)
+        nc.vector.tensor_copy(out=skip[:], in_=skip_bf[:])
+
+        params_ps = psum.tile([P, P], F32, tag="bank")
+        nc.tensor.transpose(out=params_ps[:], in_=params[:].bitcast(F32), identity=ident_f32[:])
+        gn_wb = keep.tile([P, 16, 2], F32)
+        nc.vector.tensor_copy(
+            out=gn_wb[:].rearrange("p b e -> p (b e)"), in_=params_ps[:, 0:16].bitcast(BF16)
+        )
+
+        h_codes = keep.tile([P, PASSES, S], U32, align_bytes=64)
+        h_scales = keep.tile([P, PASSES, S], U8, align_bytes=64)
+        w_codes = keep.tile([P, PASSES, DM], U32, align_bytes=64)
+        w_scales = keep.tile([P, PASSES, DM], U8, align_bytes=64)
+        stats_ps = stats_bank.tile([P, PASSES, 8], F32)
+        sum_part = [keep.tile([P, GROUPS_PER_PASS], F32, name="sum_part%d" % g) for g in range(PASSES)]
+        sumsq_part = [keep.tile([P, GROUPS_PER_PASS], F32, name="sumsq_part%d" % g) for g in range(PASSES)]
+        pair = [P, GROUPS_PER_PASS, 2]
+        gain = [keep.tile(pair, F32, name="gain%d" % g) for g in range(PASSES)]
+        shift = [keep.tile(pair, F32, name="shift%d" % g) for g in range(PASSES)]
+
+        def sums(g):
+            blocks = [(half, j) for half in range(GROUP // P) for j in range(ROW_TILES)]
+            for u in range(GROUPS_PER_PASS):
+                for i, (half, j) in enumerate(blocks):
+                    first = u * GROUP + half * P
+                    nc.tensor.matmul(
+                        out=stats_ps[:, g, 2 * u : 2 * u + 2],
+                        lhsT=h_raw[g][:, j, first : first + P],
+                        rhs=ones_bf[:],
+                        start=(i == 0),
+                        stop=(i == len(blocks) - 1),
+                    )
+
+        def squares(g):
+            for u in range(GROUPS_PER_PASS):
+                scratch = stage.tile([P, ROW_TILES, GROUP], BF16, name="scratch")
+                nc.scalar.activation(
+                    out=scratch[:],
+                    in_=h_raw[g][:, :, u * GROUP : (u + 1) * GROUP],
+                    func=ACT.Square,
+                    accum_out=sumsq_part[g][:, u : u + 1],
+                )
+
+        def copy_sums(g):
+            nc.vector.tensor_copy(out=sum_part[g][:], in_=stats_ps[:, g, 0:4:2])
+
+        def totals(g):
+            nc.tensor.matmul(out=stats_ps[:, g, 4:6], lhsT=minus_mean_of[:], rhs=sum_part[g][:], start=True, stop=True)
+            nc.tensor.matmul(out=stats_ps[:, g, 6:8], lhsT=mean_of[:], rhs=sumsq_part[g][:], start=True, stop=True)
+
+        def gain_and_shift(g):
+            moments = small.tile([P, 2 * GROUPS_PER_PASS], F32, name="moments")
+            nc.vector.tensor_copy(out=moments[:], in_=stats_ps[:, g, 4:8])
+            minus_mean = moments[:, 0:GROUPS_PER_PASS]
+            var = small.tile([P, GROUPS_PER_PASS], F32, name="var")
+            rstd = small.tile([P, GROUPS_PER_PASS], F32, name="rstd")
+            b0 = g * GROUPS_PER_PASS
+            nc.gpsimd.tensor_tensor(out=var[:], in0=minus_mean, in1=minus_mean, op=ALU.mult)
+            nc.gpsimd.tensor_tensor(out=var[:], in0=moments[:, GROUPS_PER_PASS:], in1=var[:], op=ALU.subtract)
+            nc.gpsimd.tensor_scalar(out=var[:], in0=var[:], scalar1=1.0, scalar2=EPS_GN, op0=ALU.mult, op1=ALU.add)
+            nc.gpsimd.tensor_tensor(out=rstd[:], in0=var[:], in1=minus_half[:], op=ALU.pow)
+            nc.gpsimd.tensor_tensor(
+                out=gain[g][:], in0=gn_wb[:, b0 : b0 + 2, :], in1=rstd[:].unsqueeze(2).to_broadcast(pair), op=ALU.mult
+            )
+            nc.gpsimd.tensor_tensor(
+                out=shift[g][:], in0=gain[g][:], in1=minus_mean.unsqueeze(2).to_broadcast(pair), op=ALU.mult
+            )
+            nc.gpsimd.tensor_tensor(out=shift[g][:], in0=shift[g][:], in1=gn_wb[:, 8 + b0 : 8 + b0 + 2, :], op=ALU.add)
+
+        def transpose_activations(g):
+            pairs = h_raw[g][:].rearrange("p j (u q e) -> p j u q e", u=2, e=2)
+            banks = []
+            for u in range(2):
+                for e in range(2):
+                    hT_ps = psum.tile([P, ROW_TILES, P], BF16, tag="bank", name="hT_ps")
+                    for j in range(ROW_TILES):
+                        nc.tensor.transpose(out=hT_ps[:, j, :], in_=pairs[:, j, u, :, e], identity=ident_bf[:])
+                    banks.append(hT_ps)
+            return banks
+
+        def normalise(g, banks):
+            planes = stage.tile([P, PACK, S], BF16, name="planes")
+            for t in range(PACK):
+                u, e = t // 2, t % 2
+                nc.vector.tensor_scalar(
+                    out=planes[:, t, :],
+                    in0=banks[t][:].rearrange("p j r -> p (j r)"),
+                    scalar1=gain[g][:, u, e : e + 1],
+                    scalar2=shift[g][:, u, e : e + 1],
+                    op0=ALU.mult,
+                    op1=ALU.add,
+                )
+            return planes
+
+        def regroup(planes):
+            grouped = stage.tile([P, S, PACK], BF16, align_bytes=64, name="h_grouped")
+            nc.vector.tensor_copy(
+                out=grouped[:].rearrange("p (c i) t -> p c t i", i=4),
+                in_=planes[:].rearrange("p t (c i) -> p c t i", i=4),
+            )
+            return grouped
+
+        def quantise_activations(g, grouped):
+            nc.vector.quantize_mx(
+                out=h_codes[:, g, :].bitcast(FP8X4),
+                scales=h_scales[:, g, :],
+                in_=grouped[:].rearrange("p s t -> p (s t)"),
+            )
+
+        def transpose_weights(g):
+            grouped = keep.tile([P, DM * PACK], BF16, align_bytes=64, name="w_grouped%d" % g)
+            grouped_words = grouped[:].bitcast(F32).rearrange("p (a c m u) -> p a c m u", a=W_TILES // 2, c=2, u=2)
+            for a in range(W_TILES // 2):
+                wT_ps = psum.tile([P, 2, 2, P], F32, tag="bank", name="wT_ps")
+                for c in range(2):
+                    words = w_raw[g][:, 2 * a + c, :].bitcast(F32)
+                    for u in range(2):
+                        nc.tensor.transpose(out=wT_ps[:, c, u, :], in_=words[:, u * P : (u + 1) * P], identity=ident_f32[:])
+                nc.scalar.copy(out=grouped_words[:, a], in_=wT_ps[:].rearrange("p c u m -> p c m u"))
+            return grouped
+
+        def quantise_weights(g, grouped):
+            nc.vector.quantize_mx(out=w_codes[:, g, :].bitcast(FP8X4), scales=w_scales[:, g, :], in_=grouped[:])
+
+        def multiply(acc, tile_index, g):
+            j, n = tile_index // N_HALVES, tile_index % N_HALVES
+            rows = slice(j * P, (j + 1) * P)
+            cols = slice(n * N_TILE, (n + 1) * N_TILE)
+            nc.tensor.matmul_mx(
+                out=acc[:],
+                lhsT=h_codes[:, g, rows].bitcast(FP8X4),
+                lhsT_scale=h_scales[:, g, rows],
+                rhs=w_codes[:, g, cols].bitcast(FP8X4),
+                rhs_scale=w_scales[:, g, cols],
+                start=(g == 0),
+                stop=(g == PASSES - 1),
+            )
+
+        def finish(acc, tile_index):
+            j, n = tile_index // N_HALVES, tile_index % N_HALVES
+            cols = slice(n * N_TILE, (n + 1) * N_TILE)
+            result = results.tile([P, N_TILE], F32, name="result")
+            nc.vector.scalar_tensor_tensor(
+                out=result[:], in0=x_sb[:, j, cols], scalar=skip[:, 0:1], in1=acc[:], op0=ALU.mult, op1=ALU.add
+            )
+            nc.sync.dma_start(out=out_rows[:, j, cols], in_=result[:])
+
+        sums(0)
+        squares(0)
+        copy_sums(0)
+        totals(0)
+        gain_and_shift(0)
+        banks = transpose_activations(0)
+        sums(1)
+        squares(1)
+
+        w_grouped = []
+        for g in range(PASSES - 1):
+            copy_sums(g + 1)
+            totals(g + 1)
+            planes = normalise(g, banks)
+            gain_and_shift(g + 1)
+            banks = transpose_activations(g + 1)
+            if g + 2 < PASSES:
+                sums(g + 2)
+                squares(g + 2)
+            grouped = regroup(planes)
+            quantise_activations(g, grouped)
+
+        for g in range(2):
+            w_grouped.append(transpose_weights(g))
+        quantise_weights(0, w_grouped[0])
+        planes = normalise(PASSES - 1, banks)
+        for g in range(2, PASSES):
+            w_grouped.append(transpose_weights(g))
+        quantise_weights(1, w_grouped[1])
+        grouped = regroup(planes)
+        quantise_weights(2, w_grouped[2])
+        quantise_activations(PASSES - 1, grouped)
+        quantise_weights(3, w_grouped[3])
+
+        open_accs = [psum.tile([P, N_TILE], F32, tag="bank", name="acc") for i in range(OPEN_TILES)]
+        for g in range(PASSES):
+            for i in range(OPEN_TILES):
+                multiply(open_accs[i], i, g)
+        for i in range(OPEN_TILES):
+            finish(open_accs[i], i)
+        for i in range(OPEN_TILES, ROW_TILES * N_HALVES):
+            acc = psum.tile([P, N_TILE], F32, tag="bank", name="acc")
+            for g in range(PASSES):
+                multiply(acc, i, g)
+            finish(acc, i)

@@ -26,6 +26,7 @@ W_TILES = DM // P
 N_TILE = 512
 N_HALVES = DM // N_TILE
 PSUM_BANKS = 8
+FIRST_SHARED_PASS = 2
 OPEN_TILES = PSUM_BANKS - 1
 
 FLOPS = 2 * S * DM * DI
@@ -90,7 +91,10 @@ def tile_mlstmblock_pb_kernel(tc, h_attn, gn_w, gn_b, W_out, x, skip_scale, out)
         w_scales = keep.tile([P, PASSES, DM], U8, align_bytes=64)
         stats_ps = stats_bank.tile([P, PASSES, 8], F32)
         sum_part = [keep.tile([P, GROUPS_PER_PASS], F32, name="sum_part%d" % g) for g in range(PASSES)]
-        sumsq_part = [keep.tile([P, GROUPS_PER_PASS], F32, name="sumsq_part%d" % g) for g in range(PASSES)]
+        sumsq_part = [
+            [keep.tile([P, 1], F32, name="sumsq_part%d_%d" % (g, u)) for u in range(GROUPS_PER_PASS)]
+            for g in range(PASSES)
+        ]
         pair = [P, GROUPS_PER_PASS, 2]
         gain = [keep.tile(pair, F32, name="gain%d" % g) for g in range(PASSES)]
         shift = [keep.tile(pair, F32, name="shift%d" % g) for g in range(PASSES)]
@@ -108,22 +112,32 @@ def tile_mlstmblock_pb_kernel(tc, h_attn, gn_w, gn_b, W_out, x, skip_scale, out)
                         stop=(i == len(blocks) - 1),
                     )
 
-        def squares(g):
-            for u in range(GROUPS_PER_PASS):
-                scratch = stage.tile([P, ROW_TILES, GROUP], BF16, name="scratch")
-                nc.scalar.activation(
-                    out=scratch[:],
-                    in_=h_raw[g][:, :, u * GROUP : (u + 1) * GROUP],
-                    func=ACT.Square,
-                    accum_out=sumsq_part[g][:, u : u + 1],
-                )
+        def squares_on_scalar(g, u):
+            scratch = stage.tile([P, ROW_TILES, GROUP], BF16, name="scratch_s")
+            nc.scalar.activation(
+                out=scratch[:],
+                in_=h_raw[g][:, :, u * GROUP : (u + 1) * GROUP],
+                func=ACT.Square,
+                accum_out=sumsq_part[g][u][:],
+            )
+
+        def squares_on_vector(g, u):
+            group = h_raw[g][:, :, u * GROUP : (u + 1) * GROUP]
+            scratch = stage.tile([P, ROW_TILES, GROUP], BF16, name="scratch_v")
+            nc.vector.scalar_tensor_tensor(
+                out=scratch[:], in0=group, scalar=1.0, in1=group, op0=ALU.mult, op1=ALU.mult,
+                accum_out=sumsq_part[g][u][:],
+            )
 
         def copy_sums(g):
             nc.vector.tensor_copy(out=sum_part[g][:], in_=stats_ps[:, g, 0:4:2])
 
         def totals(g):
             nc.tensor.matmul(out=stats_ps[:, g, 4:6], lhsT=minus_mean_of[:], rhs=sum_part[g][:], start=True, stop=True)
-            nc.tensor.matmul(out=stats_ps[:, g, 6:8], lhsT=mean_of[:], rhs=sumsq_part[g][:], start=True, stop=True)
+            for u in range(GROUPS_PER_PASS):
+                nc.tensor.matmul(
+                    out=stats_ps[:, g, 6 + u : 7 + u], lhsT=mean_of[:], rhs=sumsq_part[g][u][:], start=True, stop=True
+                )
 
         def gain_and_shift(g):
             moments = small.tile([P, 2 * GROUPS_PER_PASS], F32, name="moments")
@@ -155,19 +169,22 @@ def tile_mlstmblock_pb_kernel(tc, h_attn, gn_w, gn_b, W_out, x, skip_scale, out)
                     banks.append(hT_ps)
             return banks
 
-        def normalise(g, banks):
-            planes = stage.tile([P, PACK, S], BF16, name="planes")
-            for t in range(PACK):
-                u, e = t // 2, t % 2
-                nc.vector.tensor_scalar(
-                    out=planes[:, t, :],
-                    in0=banks[t][:].rearrange("p j r -> p (j r)"),
-                    scalar1=gain[g][:, u, e : e + 1],
-                    scalar2=shift[g][:, u, e : e + 1],
-                    op0=ALU.mult,
-                    op1=ALU.add,
+        def normalise(g, banks, planes, t, on_scalar):
+            u, e = t // 2, t % 2
+            bank = banks[t][:].rearrange("p j r -> p (j r)")
+            if on_scalar:
+                nc.scalar.activation(
+                    out=planes[:, t, :], in_=bank, func=ACT.Identity,
+                    scale=gain[g][:, u, e : e + 1], bias=shift[g][:, u, e : e + 1],
                 )
-            return planes
+            else:
+                nc.vector.tensor_scalar(
+                    out=planes[:, t, :], in0=bank, scalar1=gain[g][:, u, e : e + 1],
+                    scalar2=shift[g][:, u, e : e + 1], op0=ALU.mult, op1=ALU.add,
+                )
+
+        def vector_planes(g):
+            return PACK if g < FIRST_SHARED_PASS else PACK // 2
 
         def regroup(planes):
             grouped = stage.tile([P, S, PACK], BF16, align_bytes=64, name="h_grouped")
@@ -223,38 +240,53 @@ def tile_mlstmblock_pb_kernel(tc, h_attn, gn_w, gn_b, W_out, x, skip_scale, out)
             nc.sync.dma_start(out=out_rows[:, j, cols], in_=result[:])
 
         sums(0)
-        squares(0)
+        banks = transpose_activations(0)
+        squares_on_scalar(0, 0)
+        squares_on_vector(0, 1)
         copy_sums(0)
         totals(0)
         gain_and_shift(0)
-        banks = transpose_activations(0)
         sums(1)
-        squares(1)
+        squares_on_scalar(1, 0)
+        squares_on_vector(1, 1)
+        copy_sums(1)
+        totals(1)
+        planes = stage.tile([P, PACK, S], BF16, name="planes")
 
-        w_grouped = []
-        for g in range(PASSES - 1):
-            copy_sums(g + 1)
-            totals(g + 1)
-            planes = normalise(g, banks)
-            gain_and_shift(g + 1)
-            banks = transpose_activations(g + 1)
+        w_grouped = {}
+        for g in range(PASSES):
             if g + 2 < PASSES:
                 sums(g + 2)
-                squares(g + 2)
+                squares_on_scalar(g + 2, 0)
+                squares_on_scalar(g + 2, 1)
+            if g + 1 < PASSES:
+                gain_and_shift(g + 1)
+            for t in range(vector_planes(g)):
+                normalise(g, banks, planes, t, False)
+            if g + 2 < PASSES:
+                copy_sums(g + 2)
+            if g + 1 < PASSES:
+                next_banks = transpose_activations(g + 1)
+                next_planes = stage.tile([P, PACK, S], BF16, name="planes")
+                for t in range(vector_planes(g + 1), PACK):
+                    normalise(g + 1, next_banks, next_planes, t, True)
+            if g + 2 < PASSES:
+                totals(g + 2)
+            for k in range(PASSES):
+                if min(k + 1, PASSES - 1) == g:
+                    w_grouped[k] = transpose_weights(k)
+            ready = [k for k in range(PASSES) if min(k + 2, PASSES - 1) == g]
+            if len(ready) > 1:
+                quantise_weights(ready[0], w_grouped[ready[0]])
+                ready = ready[1:]
             grouped = regroup(planes)
+            if ready:
+                quantise_weights(ready[0], w_grouped[ready[0]])
             quantise_activations(g, grouped)
-
-        for g in range(2):
-            w_grouped.append(transpose_weights(g))
-        quantise_weights(0, w_grouped[0])
-        planes = normalise(PASSES - 1, banks)
-        for g in range(2, PASSES):
-            w_grouped.append(transpose_weights(g))
-        quantise_weights(1, w_grouped[1])
-        grouped = regroup(planes)
-        quantise_weights(2, w_grouped[2])
-        quantise_activations(PASSES - 1, grouped)
-        quantise_weights(3, w_grouped[3])
+            for k in ready[1:]:
+                quantise_weights(k, w_grouped[k])
+            if g + 1 < PASSES:
+                banks, planes = next_banks, next_planes
 
         open_accs = [psum.tile([P, N_TILE], F32, tag="bank", name="acc") for i in range(OPEN_TILES)]
         for g in range(PASSES):

@@ -67,8 +67,6 @@ def tile_mlstmblock_pb_kernel(tc, h_attn, gn_w, gn_b, W_out, x, skip_scale, out)
         make_identity(nc, ident_f32[:])
         ident_bf = keep.tile([P, P], BF16)
         make_identity(nc, ident_bf[:])
-        ones_bf = keep.tile([P, 2], BF16)
-        nc.vector.memset(ones_bf[:], 1.0)
         minus_mean_of = keep.tile([P, P], F32)
         nc.vector.memset(minus_mean_of[:], -1.0 / (S * GROUP))
         mean_of = keep.tile([P, P], F32)
@@ -89,7 +87,7 @@ def tile_mlstmblock_pb_kernel(tc, h_attn, gn_w, gn_b, W_out, x, skip_scale, out)
         h_scales = keep.tile([P, PASSES, S], U8, align_bytes=64)
         w_codes = keep.tile([P, PASSES, DM], U32, align_bytes=64)
         w_scales = keep.tile([P, PASSES, DM], U8, align_bytes=64)
-        stats_ps = stats_bank.tile([P, PASSES, 8], F32)
+        stats_ps = stats_bank.tile([P, PASSES, 4], F32)
         sum_part = [keep.tile([P, GROUPS_PER_PASS], F32, name="sum_part%d" % g) for g in range(PASSES)]
         sumsq_part = [
             [keep.tile([P, 1], F32, name="sumsq_part%d_%d" % (g, u)) for u in range(GROUPS_PER_PASS)]
@@ -100,17 +98,17 @@ def tile_mlstmblock_pb_kernel(tc, h_attn, gn_w, gn_b, W_out, x, skip_scale, out)
         shift = [keep.tile(pair, F32, name="shift%d" % g) for g in range(PASSES)]
 
         def sums(g):
-            blocks = [(half, j) for half in range(GROUP // P) for j in range(ROW_TILES)]
             for u in range(GROUPS_PER_PASS):
-                for i, (half, j) in enumerate(blocks):
-                    first = u * GROUP + half * P
-                    nc.tensor.matmul(
-                        out=stats_ps[:, g, 2 * u : 2 * u + 2],
-                        lhsT=h_raw[g][:, j, first : first + P],
-                        rhs=ones_bf[:],
-                        start=(i == 0),
-                        stop=(i == len(blocks) - 1),
-                    )
+                scratch = stage.tile([P, ROW_TILES, GROUP], BF16, name="scratch_v")
+                nc.vector.tensor_scalar(
+                    out=scratch[:],
+                    in0=h_raw[g][:, :, u * GROUP : (u + 1) * GROUP],
+                    scalar1=1.0,
+                    scalar2=None,
+                    op0=ALU.mult,
+                    op1=ALU.add,
+                    accum_out=sum_part[g][:, u : u + 1],
+                )
 
         def squares_on_scalar(g, u):
             scratch = stage.tile([P, ROW_TILES, GROUP], BF16, name="scratch_s")
@@ -129,19 +127,16 @@ def tile_mlstmblock_pb_kernel(tc, h_attn, gn_w, gn_b, W_out, x, skip_scale, out)
                 accum_out=sumsq_part[g][u][:],
             )
 
-        def copy_sums(g):
-            nc.vector.tensor_copy(out=sum_part[g][:], in_=stats_ps[:, g, 0:4:2])
-
         def totals(g):
-            nc.tensor.matmul(out=stats_ps[:, g, 4:6], lhsT=minus_mean_of[:], rhs=sum_part[g][:], start=True, stop=True)
+            nc.tensor.matmul(out=stats_ps[:, g, 0:2], lhsT=minus_mean_of[:], rhs=sum_part[g][:], start=True, stop=True)
             for u in range(GROUPS_PER_PASS):
                 nc.tensor.matmul(
-                    out=stats_ps[:, g, 6 + u : 7 + u], lhsT=mean_of[:], rhs=sumsq_part[g][u][:], start=True, stop=True
+                    out=stats_ps[:, g, 2 + u : 3 + u], lhsT=mean_of[:], rhs=sumsq_part[g][u][:], start=True, stop=True
                 )
 
         def gain_and_shift(g):
             moments = small.tile([P, 2 * GROUPS_PER_PASS], F32, name="moments")
-            nc.vector.tensor_copy(out=moments[:], in_=stats_ps[:, g, 4:8])
+            nc.vector.tensor_copy(out=moments[:], in_=stats_ps[:, g, :])
             minus_mean = moments[:, 0:GROUPS_PER_PASS]
             var = small.tile([P, GROUPS_PER_PASS], F32, name="var")
             rstd = small.tile([P, GROUPS_PER_PASS], F32, name="rstd")
@@ -239,24 +234,21 @@ def tile_mlstmblock_pb_kernel(tc, h_attn, gn_w, gn_b, W_out, x, skip_scale, out)
             )
             nc.sync.dma_start(out=out_rows[:, j, cols], in_=result[:])
 
-        sums(0)
         banks = transpose_activations(0)
+        sums(0)
         squares_on_scalar(0, 0)
         squares_on_vector(0, 1)
-        copy_sums(0)
         totals(0)
         gain_and_shift(0)
         sums(1)
         squares_on_scalar(1, 0)
-        squares_on_vector(1, 1)
-        copy_sums(1)
+        squares_on_scalar(1, 1)
         totals(1)
         planes = stage.tile([P, PACK, S], BF16, name="planes")
 
         w_grouped = {}
         for g in range(PASSES):
             if g + 2 < PASSES:
-                sums(g + 2)
                 squares_on_scalar(g + 2, 0)
                 squares_on_scalar(g + 2, 1)
             if g + 1 < PASSES:
@@ -264,7 +256,7 @@ def tile_mlstmblock_pb_kernel(tc, h_attn, gn_w, gn_b, W_out, x, skip_scale, out)
             for t in range(vector_planes(g)):
                 normalise(g, banks, planes, t, False)
             if g + 2 < PASSES:
-                copy_sums(g + 2)
+                sums(g + 2)
             if g + 1 < PASSES:
                 next_banks = transpose_activations(g + 1)
                 next_planes = stage.tile([P, PACK, S], BF16, name="planes")

@@ -27,6 +27,11 @@ N_TILE = 512
 N_HALVES = DM // N_TILE
 PSUM_BANKS = 8
 FIRST_SHARED_PASS = 2
+UNIT_TILES = 4
+UNIT_ROWS = UNIT_TILES * P
+UNITS_PER_PASS = ROW_TILES // UNIT_TILES
+UNITS = PASSES * UNITS_PER_PASS
+FIRST_W_UNIT = 3
 OPEN_TILES = PSUM_BANKS - 1
 
 FLOPS = 2 * S * DM * DI
@@ -52,8 +57,6 @@ def tile_mlstmblock_pb_kernel(tc, h_attn, gn_w, gn_b, W_out, x, skip_scale, out)
         nc.vector.memset(params[:], 0.0)
         nc.sync.dma_start(out=params[0:8, :], in_=gn_w.rearrange("(b c) -> b c", c=GROUP))
         nc.sync.dma_start(out=params[8:16, :], in_=gn_b.rearrange("(b c) -> b c", c=GROUP))
-        skip_bf = keep.tile([P, 1], BF16)
-        nc.sync.dma_start(out=skip_bf[:], in_=skip_scale.partition_broadcast(P))
         h_raw = [keep.tile([P, ROW_TILES, K_PASS], BF16, name="h_raw%d" % g) for g in range(PASSES)]
         w_raw = [keep.tile([P, W_TILES, K_PASS], BF16, name="w_raw%d" % g) for g in range(PASSES)]
         for g in range(PASSES):
@@ -62,6 +65,8 @@ def tile_mlstmblock_pb_kernel(tc, h_attn, gn_w, gn_b, W_out, x, skip_scale, out)
             nc.sync.dma_start(out=w_raw[g][:], in_=w_rows[:, :, g * K_PASS : (g + 1) * K_PASS])
         x_sb = keep.tile([P, ROW_TILES, DM], BF16)
         nc.sync.dma_start(out=x_sb[:], in_=x_rows)
+        skip_bf = keep.tile([P, 1], BF16)
+        nc.sync.dma_start(out=skip_bf[:], in_=skip_scale.partition_broadcast(P))
 
         ident_f32 = keep.tile([P, P], F32)
         make_identity(nc, ident_f32[:])
@@ -73,8 +78,6 @@ def tile_mlstmblock_pb_kernel(tc, h_attn, gn_w, gn_b, W_out, x, skip_scale, out)
         nc.vector.memset(mean_of[:], 1.0 / (S * GROUP))
         minus_half = keep.tile([P, GROUPS_PER_PASS], F32)
         nc.vector.memset(minus_half[:], -0.5)
-        skip = keep.tile([P, 1], F32)
-        nc.vector.tensor_copy(out=skip[:], in_=skip_bf[:])
 
         params_ps = psum.tile([P, P], F32, tag="bank")
         nc.tensor.transpose(out=params_ps[:], in_=params[:].bitcast(F32), identity=ident_f32[:])
@@ -153,20 +156,22 @@ def tile_mlstmblock_pb_kernel(tc, h_attn, gn_w, gn_b, W_out, x, skip_scale, out)
             )
             nc.gpsimd.tensor_tensor(out=shift[g][:], in0=shift[g][:], in1=gn_wb[:, 8 + b0 : 8 + b0 + 2, :], op=ALU.add)
 
-        def transpose_activations(g):
+        def transpose_activations(g, r):
             pairs = h_raw[g][:].rearrange("p j (u q e) -> p j u q e", u=2, e=2)
             banks = []
             for u in range(2):
                 for e in range(2):
-                    hT_ps = psum.tile([P, ROW_TILES, P], BF16, tag="bank", name="hT_ps")
-                    for j in range(ROW_TILES):
-                        nc.tensor.transpose(out=hT_ps[:, j, :], in_=pairs[:, j, u, :, e], identity=ident_bf[:])
+                    hT_ps = psum.tile([P, UNIT_TILES, P], BF16, tag="bank", name="hT_ps")
+                    for i in range(UNIT_TILES):
+                        nc.tensor.transpose(
+                            out=hT_ps[:, i, :], in_=pairs[:, r * UNIT_TILES + i, u, :, e], identity=ident_bf[:]
+                        )
                     banks.append(hT_ps)
             return banks
 
         def normalise(g, banks, planes, t, on_scalar):
             u, e = t // 2, t % 2
-            bank = banks[t][:].rearrange("p j r -> p (j r)")
+            bank = banks[t][:].rearrange("p i r -> p (i r)")
             if on_scalar:
                 nc.scalar.activation(
                     out=planes[:, t, :], in_=bank, func=ACT.Identity,
@@ -182,17 +187,18 @@ def tile_mlstmblock_pb_kernel(tc, h_attn, gn_w, gn_b, W_out, x, skip_scale, out)
             return PACK if g < FIRST_SHARED_PASS else PACK // 2
 
         def regroup(planes):
-            grouped = stage.tile([P, S, PACK], BF16, align_bytes=64, name="h_grouped")
+            grouped = stage.tile([P, UNIT_ROWS, PACK], BF16, align_bytes=64, name="h_grouped")
             nc.vector.tensor_copy(
                 out=grouped[:].rearrange("p (c i) t -> p c t i", i=4),
                 in_=planes[:].rearrange("p t (c i) -> p c t i", i=4),
             )
             return grouped
 
-        def quantise_activations(g, grouped):
+        def quantise_activations(g, r, grouped):
+            rows = slice(r * UNIT_ROWS, (r + 1) * UNIT_ROWS)
             nc.vector.quantize_mx(
-                out=h_codes[:, g, :].bitcast(FP8X4),
-                scales=h_scales[:, g, :],
+                out=h_codes[:, g, rows].bitcast(FP8X4),
+                scales=h_scales[:, g, rows],
                 in_=grouped[:].rearrange("p s t -> p (s t)"),
             )
 
@@ -234,7 +240,7 @@ def tile_mlstmblock_pb_kernel(tc, h_attn, gn_w, gn_b, W_out, x, skip_scale, out)
             )
             nc.sync.dma_start(out=out_rows[:, j, cols], in_=result[:])
 
-        banks = transpose_activations(0)
+        banks = transpose_activations(0, 0)
         sums(0)
         squares_on_scalar(0, 0)
         squares_on_vector(0, 1)
@@ -244,41 +250,39 @@ def tile_mlstmblock_pb_kernel(tc, h_attn, gn_w, gn_b, W_out, x, skip_scale, out)
         squares_on_scalar(1, 0)
         squares_on_scalar(1, 1)
         totals(1)
-        planes = stage.tile([P, PACK, S], BF16, name="planes")
+        planes = stage.tile([P, PACK, UNIT_ROWS], BF16, name="planes")
 
         w_grouped = {}
-        for g in range(PASSES):
-            if g + 2 < PASSES:
+        for k in range(UNITS):
+            g, r = k // UNITS_PER_PASS, k % UNITS_PER_PASS
+            new_pass = r == 0
+            if new_pass and g + 2 < PASSES:
                 squares_on_scalar(g + 2, 0)
                 squares_on_scalar(g + 2, 1)
-            if g + 1 < PASSES:
+            if new_pass and g + 1 < PASSES:
                 gain_and_shift(g + 1)
             for t in range(vector_planes(g)):
                 normalise(g, banks, planes, t, False)
-            if g + 2 < PASSES:
+            if new_pass and g + 2 < PASSES:
                 sums(g + 2)
-            if g + 1 < PASSES:
-                next_banks = transpose_activations(g + 1)
-                next_planes = stage.tile([P, PACK, S], BF16, name="planes")
-                for t in range(vector_planes(g + 1), PACK):
-                    normalise(g + 1, next_banks, next_planes, t, True)
-            if g + 2 < PASSES:
+            if k + 1 < UNITS:
+                next_g, next_r = (k + 1) // UNITS_PER_PASS, (k + 1) % UNITS_PER_PASS
+                next_banks = transpose_activations(next_g, next_r)
+                next_planes = stage.tile([P, PACK, UNIT_ROWS], BF16, name="planes")
+                for t in range(vector_planes(next_g), PACK):
+                    normalise(next_g, next_banks, next_planes, t, True)
+            if new_pass and g + 2 < PASSES:
                 totals(g + 2)
-            for k in range(PASSES):
-                if min(k + 1, PASSES - 1) == g:
-                    w_grouped[k] = transpose_weights(k)
-            ready = [k for k in range(PASSES) if min(k + 2, PASSES - 1) == g]
-            if len(ready) > 1:
-                quantise_weights(ready[0], w_grouped[ready[0]])
-                ready = ready[1:]
+            if 0 <= k - FIRST_W_UNIT < PASSES:
+                w_grouped[k - FIRST_W_UNIT] = transpose_weights(k - FIRST_W_UNIT)
             grouped = regroup(planes)
-            if ready:
-                quantise_weights(ready[0], w_grouped[ready[0]])
-            quantise_activations(g, grouped)
-            for k in ready[1:]:
-                quantise_weights(k, w_grouped[k])
-            if g + 1 < PASSES:
+            if 0 <= k - FIRST_W_UNIT - 1 < PASSES:
+                quantise_weights(k - FIRST_W_UNIT - 1, w_grouped[k - FIRST_W_UNIT - 1])
+            quantise_activations(g, r, grouped)
+            if k + 1 < UNITS:
                 banks, planes = next_banks, next_planes
+        skip = keep.tile([P, 1], F32)
+        nc.vector.tensor_copy(out=skip[:], in_=skip_bf[:])
 
         open_accs = [psum.tile([P, N_TILE], F32, tag="bank", name="acc") for i in range(OPEN_TILES)]
         for g in range(PASSES):

from contextlib import ExitStack

import concourse.mybir as mybir
from concourse.masks import make_identity

F32 = mybir.dt.float32
BF16 = mybir.dt.bfloat16
U32 = mybir.dt.uint32
U8 = mybir.dt.uint8
FP8X4 = mybir.dt.float8_e4m3fn_x4
ALU = mybir.AluOpType
ACT = mybir.ActivationFunctionType

P = 128
PACK = 4
K_PASS = P * PACK
S = 1024
DI = 2048
DM = 1024
GROUP = 256
EPS_GN = 1e-5
PASSES = DI // K_PASS
GROUPS_PER_PASS = K_PASS // GROUP
ROW_TILES = S // P
W_TILES = DM // P
N_TILE = 512
N_HALVES = DM // N_TILE
PSUM_BANKS = 8
FIRST_SHARED_PASS = 2
UNIT_TILES = 4
UNIT_ROWS = UNIT_TILES * P
UNITS_PER_PASS = ROW_TILES // UNIT_TILES
UNITS = PASSES * UNITS_PER_PASS
FIRST_W_UNIT = 3
OPEN_TILES = PSUM_BANKS - 1

FLOPS = 2 * S * DM * DI


def tile_mlstmblock_pb_kernel(tc, h_attn, gn_w, gn_b, W_out, x, skip_scale, out):
    nc = tc.nc
    h_rows = h_attn.flatten_outer_dims().rearrange("(p j) c -> p j c", j=ROW_TILES)
    x_rows = x.flatten_outer_dims().rearrange("(p j) m -> p j m", j=ROW_TILES)
    out_rows = out.flatten_outer_dims().rearrange("(p j) m -> p j m", j=ROW_TILES)
    w_rows = W_out.rearrange("(t p) c -> p t c", p=P)

    with ExitStack() as ctx:
        ctx.enter_context(tc.manual_schedule())
        keep = ctx.enter_context(tc.tile_pool(name="keep", bufs=1))
        small = ctx.enter_context(tc.tile_pool(name="small", bufs=2))
        stage = ctx.enter_context(tc.tile_pool(name="stage", bufs=2))
        results = ctx.enter_context(tc.tile_pool(name="results", bufs=4))
        stats_bank = ctx.enter_context(tc.psum_pool(name="stats_bank", bufs=1))
        psum = ctx.enter_context(tc.psum_pool(name="psum", bufs=PSUM_BANKS - 1))

        params = keep.tile([P, 2 * P], BF16)
        nc.vector.memset(params[:], 0.0)
        nc.sync.dma_start(out=params[0:8, :], in_=gn_w.rearrange("(b c) -> b c", c=GROUP))
        nc.sync.dma_start(out=params[8:16, :], in_=gn_b.rearrange("(b c) -> b c", c=GROUP))
        h_raw = [keep.tile([P, ROW_TILES, K_PASS], BF16, name="h_raw%d" % g) for g in range(PASSES)]
        w_raw = [keep.tile([P, W_TILES, K_PASS], BF16, name="w_raw%d" % g) for g in range(PASSES)]
        for g in range(PASSES):
            nc.sync.dma_start(out=h_raw[g][:], in_=h_rows[:, :, g * K_PASS : (g + 1) * K_PASS])
        for g in range(PASSES):
            nc.sync.dma_start(out=w_raw[g][:], in_=w_rows[:, :, g * K_PASS : (g + 1) * K_PASS])
        x_sb = keep.tile([P, ROW_TILES, DM], BF16)
        nc.sync.dma_start(out=x_sb[:], in_=x_rows)
        skip_bf = keep.tile([P, 1], BF16)
        nc.sync.dma_start(out=skip_bf[:], in_=skip_scale.partition_broadcast(P))

        ident_f32 = keep.tile([P, P], F32)
        make_identity(nc, ident_f32[:])
        ident_bf = keep.tile([P, P], BF16)
        make_identity(nc, ident_bf[:])
        minus_mean_of = keep.tile([P, P], F32)
        nc.vector.memset(minus_mean_of[:], -1.0 / (S * GROUP))
        mean_of = keep.tile([P, P], F32)
        nc.vector.memset(mean_of[:], 1.0 / (S * GROUP))
        minus_half = keep.tile([P, GROUPS_PER_PASS], F32)
        nc.vector.memset(minus_half[:], -0.5)

        params_ps = psum.tile([P, P], F32, tag="bank")
        nc.tensor.transpose(out=params_ps[:], in_=params[:].bitcast(F32), identity=ident_f32[:])
        gn_wb = keep.tile([P, 16, 2], F32)
        nc.vector.tensor_copy(
            out=gn_wb[:].rearrange("p b e -> p (b e)"), in_=params_ps[:, 0:16].bitcast(BF16)
        )

        h_codes = keep.tile([P, PASSES, S], U32, align_bytes=64)
        h_scales = keep.tile([P, PASSES, S], U8, align_bytes=64)
        w_codes = keep.tile([P, PASSES, DM], U32, align_bytes=64)
        w_scales = keep.tile([P, PASSES, DM], U8, align_bytes=64)
        stats_ps = stats_bank.tile([P, PASSES, 4], F32)
        sum_part = [keep.tile([P, GROUPS_PER_PASS], F32, name="sum_part%d" % g) for g in range(PASSES)]
        sumsq_part = [
            [keep.tile([P, 1], F32, name="sumsq_part%d_%d" % (g, u)) for u in range(GROUPS_PER_PASS)]
            for g in range(PASSES)
        ]
        pair = [P, GROUPS_PER_PASS, 2]
        gain = [keep.tile(pair, F32, name="gain%d" % g) for g in range(PASSES)]
        shift = [keep.tile(pair, F32, name="shift%d" % g) for g in range(PASSES)]

        def sums(g):
            for u in range(GROUPS_PER_PASS):
                scratch = stage.tile([P, ROW_TILES, GROUP], BF16, name="scratch_v")
                nc.vector.tensor_scalar(
                    out=scratch[:],
                    in0=h_raw[g][:, :, u * GROUP : (u + 1) * GROUP],
                    scalar1=1.0,
                    scalar2=None,
                    op0=ALU.mult,
                    op1=ALU.add,
                    accum_out=sum_part[g][:, u : u + 1],
                )

        def squares_on_scalar(g, u):
            scratch = stage.tile([P, ROW_TILES, GROUP], BF16, name="scratch_s")
            nc.scalar.activation(
                out=scratch[:],
                in_=h_raw[g][:, :, u * GROUP : (u + 1) * GROUP],
                func=ACT.Square,
                accum_out=sumsq_part[g][u][:],
            )

        def squares_on_vector(g, u):
            group = h_raw[g][:, :, u * GROUP : (u + 1) * GROUP]
            scratch = stage.tile([P, ROW_TILES, GROUP], BF16, name="scratch_v")
            nc.vector.scalar_tensor_tensor(
                out=scratch[:], in0=group, scalar=1.0, in1=group, op0=ALU.mult, op1=ALU.mult,
                accum_out=sumsq_part[g][u][:],
            )

        def totals(g):
            nc.tensor.matmul(out=stats_ps[:, g, 0:2], lhsT=minus_mean_of[:], rhs=sum_part[g][:], start=True, stop=True)
            for u in range(GROUPS_PER_PASS):
                nc.tensor.matmul(
                    out=stats_ps[:, g, 2 + u : 3 + u], lhsT=mean_of[:], rhs=sumsq_part[g][u][:], start=True, stop=True
                )

        def gain_and_shift(g):
            moments = small.tile([P, 2 * GROUPS_PER_PASS], F32, name="moments")
            nc.vector.tensor_copy(out=moments[:], in_=stats_ps[:, g, :])
            minus_mean = moments[:, 0:GROUPS_PER_PASS]
            var = small.tile([P, GROUPS_PER_PASS], F32, name="var")
            rstd = small.tile([P, GROUPS_PER_PASS], F32, name="rstd")
            b0 = g * GROUPS_PER_PASS
            nc.gpsimd.tensor_tensor(out=var[:], in0=minus_mean, in1=minus_mean, op=ALU.mult)
            nc.gpsimd.tensor_tensor(out=var[:], in0=moments[:, GROUPS_PER_PASS:], in1=var[:], op=ALU.subtract)
            nc.gpsimd.tensor_scalar(out=var[:], in0=var[:], scalar1=1.0, scalar2=EPS_GN, op0=ALU.mult, op1=ALU.add)
            nc.gpsimd.tensor_tensor(out=rstd[:], in0=var[:], in1=minus_half[:], op=ALU.pow)
            nc.gpsimd.tensor_tensor(
                out=gain[g][:], in0=gn_wb[:, b0 : b0 + 2, :], in1=rstd[:].unsqueeze(2).to_broadcast(pair), op=ALU.mult
            )
            nc.gpsimd.tensor_tensor(
                out=shift[g][:], in0=gain[g][:], in1=minus_mean.unsqueeze(2).to_broadcast(pair), op=ALU.mult
            )
            nc.gpsimd.tensor_tensor(out=shift[g][:], in0=shift[g][:], in1=gn_wb[:, 8 + b0 : 8 + b0 + 2, :], op=ALU.add)

        def transpose_activations(g, r):
            pairs = h_raw[g][:].rearrange("p j (u q e) -> p j u q e", u=2, e=2)
            banks = []
            for u in range(2):
                for e in range(2):
                    hT_ps = psum.tile([P, UNIT_TILES, P], BF16, tag="bank", name="hT_ps")
                    for i in range(UNIT_TILES):
                        nc.tensor.transpose(
                            out=hT_ps[:, i, :], in_=pairs[:, r * UNIT_TILES + i, u, :, e], identity=ident_bf[:]
                        )
                    banks.append(hT_ps)
            return banks

        def normalise(g, banks, planes, t, on_scalar):
            u, e = t // 2, t % 2
            bank = banks[t][:].rearrange("p i r -> p (i r)")
            if on_scalar:
                nc.scalar.activation(
                    out=planes[:, t, :], in_=bank, func=ACT.Identity,
                    scale=gain[g][:, u, e : e + 1], bias=shift[g][:, u, e : e + 1],
                )
            else:
                nc.vector.tensor_scalar(
                    out=planes[:, t, :], in0=bank, scalar1=gain[g][:, u, e : e + 1],
                    scalar2=shift[g][:, u, e : e + 1], op0=ALU.mult, op1=ALU.add,
                )

        def vector_planes(g):
            return PACK if g < FIRST_SHARED_PASS else PACK // 2

        def regroup(planes):
            grouped = stage.tile([P, UNIT_ROWS, PACK], BF16, align_bytes=64, name="h_grouped")
            nc.vector.tensor_copy(
                out=grouped[:].rearrange("p (c i) t -> p c t i", i=4),
                in_=planes[:].rearrange("p t (c i) -> p c t i", i=4),
            )
            return grouped

        def quantise_activations(g, r, grouped):
            rows = slice(r * UNIT_ROWS, (r + 1) * UNIT_ROWS)
            nc.vector.quantize_mx(
                out=h_codes[:, g, rows].bitcast(FP8X4),
                scales=h_scales[:, g, rows],
                in_=grouped[:].rearrange("p s t -> p (s t)"),
            )

        def transpose_weights(g):
            grouped = keep.tile([P, DM * PACK], BF16, align_bytes=64, name="w_grouped%d" % g)
            grouped_words = grouped[:].bitcast(F32).rearrange("p (a c m u) -> p a c m u", a=W_TILES // 2, c=2, u=2)
            for a in range(W_TILES // 2):
                wT_ps = psum.tile([P, 2, 2, P], F32, tag="bank", name="wT_ps")
                for c in range(2):
                    words = w_raw[g][:, 2 * a + c, :].bitcast(F32)
                    for u in range(2):
                        nc.tensor.transpose(out=wT_ps[:, c, u, :], in_=words[:, u * P : (u + 1) * P], identity=ident_f32[:])
                nc.scalar.copy(out=grouped_words[:, a], in_=wT_ps[:].rearrange("p c u m -> p c m u"))
            return grouped

        def quantise_weights(g, grouped):
            nc.vector.quantize_mx(out=w_codes[:, g, :].bitcast(FP8X4), scales=w_scales[:, g, :], in_=grouped[:])

        def multiply(acc, tile_index, g):
            j, n = tile_index // N_HALVES, tile_index % N_HALVES
            rows = slice(j * P, (j + 1) * P)
            cols = slice(n * N_TILE, (n + 1) * N_TILE)
            nc.tensor.matmul_mx(
                out=acc[:],
                lhsT=h_codes[:, g, rows].bitcast(FP8X4),
                lhsT_scale=h_scales[:, g, rows],
                rhs=w_codes[:, g, cols].bitcast(FP8X4),
                rhs_scale=w_scales[:, g, cols],
                start=(g == 0),
                stop=(g == PASSES - 1),
            )

        def finish(acc, tile_index):
            j, n = tile_index // N_HALVES, tile_index % N_HALVES
            cols = slice(n * N_TILE, (n + 1) * N_TILE)
            result = results.tile([P, N_TILE], F32, name="result")
            nc.vector.scalar_tensor_tensor(
                out=result[:], in0=x_sb[:, j, cols], scalar=skip[:, 0:1], in1=acc[:], op0=ALU.mult, op1=ALU.add
            )
            nc.sync.dma_start(out=out_rows[:, j, cols], in_=result[:])

        banks = transpose_activations(0, 0)
        sums(0)
        squares_on_scalar(0, 0)
        squares_on_vector(0, 1)
        totals(0)
        gain_and_shift(0)
        sums(1)
        squares_on_scalar(1, 0)
        squares_on_scalar(1, 1)
        totals(1)
        planes = stage.tile([P, PACK, UNIT_ROWS], BF16, name="planes")

        w_grouped = {}
        for k in range(UNITS):
            g, r = k // UNITS_PER_PASS, k % UNITS_PER_PASS
            new_pass = r == 0
            if new_pass and g + 2 < PASSES:
                squares_on_scalar(g + 2, 0)
                squares_on_scalar(g + 2, 1)
            if new_pass and g + 1 < PASSES:
                gain_and_shift(g + 1)
            for t in range(vector_planes(g)):
                normalise(g, banks, planes, t, False)
            if new_pass and g + 2 < PASSES:
                sums(g + 2)
            if k + 1 < UNITS:
                next_g, next_r = (k + 1) // UNITS_PER_PASS, (k + 1) % UNITS_PER_PASS
                next_banks = transpose_activations(next_g, next_r)
                next_planes = stage.tile([P, PACK, UNIT_ROWS], BF16, name="planes")
                for t in range(vector_planes(next_g), PACK):
                    normalise(next_g, next_banks, next_planes, t, True)
            if new_pass and g + 2 < PASSES:
                totals(g + 2)
            if 0 <= k - FIRST_W_UNIT < PASSES:
                w_grouped[k - FIRST_W_UNIT] = transpose_weights(k - FIRST_W_UNIT)
            grouped = regroup(planes)
            if 0 <= k - FIRST_W_UNIT - 1 < PASSES:
                quantise_weights(k - FIRST_W_UNIT - 1, w_grouped[k - FIRST_W_UNIT - 1])
            quantise_activations(g, r, grouped)
            if k + 1 < UNITS:
                banks, planes = next_banks, next_planes
        skip = keep.tile([P, 1], F32)
        nc.vector.tensor_copy(out=skip[:], in_=skip_bf[:])

        open_accs = [psum.tile([P, N_TILE], F32, tag="bank", name="acc") for i in range(OPEN_TILES)]
        for g in range(PASSES):
            for i in range(OPEN_TILES):
                multiply(open_accs[i], i, g)
        for i in range(OPEN_TILES):
            finish(open_accs[i], i)
        for i in range(OPEN_TILES, ROW_TILES * N_HALVES):
            acc = psum.tile([P, N_TILE], F32, tag="bank", name="acc")
            for g in range(PASSES):
                multiply(acc, i, g)
            finish(acc, i)
